import numpy as np
import ml_dtypes

BF16 = ml_dtypes.bfloat16


def bf(x):
    return np.asarray(x, np.float32).astype(BF16)


def f32(x):
    return np.asarray(x, np.float32)


def f64(x):
    return np.asarray(x).astype(np.float64)


def striped(idx):
    return np.tile(idx.reshape(-1, 16).T, (8, 1))


D, S, M, B, Q, N = 128, 4096, 512, 32, 16, 512


def setup_inputs():
    return {"table": bf(np.random.standard_normal((D, S))), "w": bf(np.random.standard_normal((D, M)) / np.sqrt(D)), "b": f32(0.1 * np.random.standard_normal((M, 1))), "offs": striped(np.random.permutation(S)[:N])}


def reference(table, w, b, offs):
    idx = offs[:16].T.reshape(-1)
    proj = f64(w).T @ f64(table)[:, idx]
    return proj.reshape(M, B, Q).sum(axis=2) / Q + f64(b)

@@ -1,0 +1,60 @@
+import concourse.mybir as mybir
+from concourse.masks import make_identity
+
+P = 128
+S = 4096
+M = 512
+N = 512
+Q = 16
+E = N // Q
+BLOCKS = M // P
+
+FLOPS = 2 * P * M * N
+
+BF16, F32, U16 = mybir.dt.bfloat16, mybir.dt.float32, mybir.dt.uint16
+MULT, ADD = mybir.AluOpType.mult, mybir.AluOpType.add
+
+
+def tile_multiscalehead_kernel(tc, table, w, b, offs, out):
+    nc = tc.nc
+    with (
+        tc.tile_pool(name="held", bufs=1) as held,
+        tc.tile_pool(name="work", bufs=BLOCKS) as work,
+        tc.psum_pool(name="bias_bank", bufs=1) as bias_bank,
+        tc.psum_pool(name="banks", bufs=BLOCKS) as banks,
+    ):
+        offsets = held.tile([P, N // 16], U16, name="offsets")
+        nc.sync.dma_start(offsets[:], offs)
+        states = held.tile([P, S], BF16, name="states")
+        nc.sync.dma_start(states[:], table)
+        weights = held.tile([P, M], BF16, name="weights")
+        nc.scalar.dma_start(weights[:], w)
+        bias_rows = held.tile([BLOCKS, P], F32, name="bias_rows")
+        nc.scalar.dma_start(bias_rows[:], b.rearrange("(t p) o -> t (p o)", p=P))
+
+        identity = held.tile([BLOCKS, BLOCKS], F32, name="identity")
+        make_identity(nc, identity[:])
+        bias_psum = bias_bank.tile([P, BLOCKS], F32, name="bias_psum")
+        nc.tensor.matmul(bias_psum[:], bias_rows[:], identity[:], start=True, stop=True)
+        bias = held.tile([P, BLOCKS], F32, name="bias")
+        nc.vector.tensor_copy(bias[:], bias_psum[:])
+
+        for t in range(BLOCKS):
+            projected = banks.tile([P, N], F32, name="projected")
+            nc.tensor.matmul(
+                projected[:],
+                weights[:, t * P : (t + 1) * P],
+                states[:].indirect(offsets[:]),
+                start=True,
+                stop=True,
+            )
+            sums = work.tile([P, E], F32, name="sums")
+            nc.vector.tensor_reduce(
+                sums[:],
+                projected[:].rearrange("p (e q) -> p e q", q=Q),
+                axis=mybir.AxisListType.X,
+                op=ADD,
+            )
+            scores = work.tile([P, E], F32, name="scores")
+            nc.vector.tensor_scalar(scores[:], sums[:], 1.0 / Q, bias[:, t : t + 1], op0=MULT, op1=ADD)
+            nc.sync.dma_start(out[t * P : (t + 1) * P, :], scores[:])

@@ -8,6 +8,7 @@ N = 512
 Q = 16
 E = N // Q
 BLOCKS = M // P
+WARM_UPS = 10
 
 FLOPS = 2 * P * M * N
 
@@ -20,7 +21,7 @@ def tile_multiscalehead_kernel(tc, table, w, b, offs, out):
     with (
         tc.tile_pool(name="held", bufs=1) as held,
         tc.tile_pool(name="work", bufs=BLOCKS) as work,
-        tc.psum_pool(name="bias_bank", bufs=1) as bias_bank,
+        tc.psum_pool(name="side_banks", bufs=1) as side_banks,
         tc.psum_pool(name="banks", bufs=BLOCKS) as banks,
     ):
         offsets = held.tile([P, N // 16], U16, name="offsets")
@@ -32,9 +33,15 @@ def tile_multiscalehead_kernel(tc, table, w, b, offs, out):
         bias_rows = held.tile([BLOCKS, P], F32, name="bias_rows")
         nc.scalar.dma_start(bias_rows[:], b.rearrange("(t p) o -> t (p o)", p=P))
 
+        zeros = held.tile([P, N], BF16, name="zeros")
+        nc.vector.memset(zeros[:], 0.0)
+        unused = side_banks.tile([P, N], F32, name="unused")
+        for i in range(WARM_UPS):
+            nc.tensor.matmul(unused[:], zeros[:, 0:P], zeros[:], start=True, stop=True)
+
         identity = held.tile([BLOCKS, BLOCKS], F32, name="identity")
         make_identity(nc, identity[:])
-        bias_psum = bias_bank.tile([P, BLOCKS], F32, name="bias_psum")
+        bias_psum = side_banks.tile([P, BLOCKS], F32, name="bias_psum")
         nc.tensor.matmul(bias_psum[:], bias_rows[:], identity[:], start=True, stop=True)
         bias = held.tile([P, BLOCKS], F32, name="bias")
         nc.vector.tensor_copy(bias[:], bias_psum[:])

@@ -8,12 +8,12 @@ N = 512
 Q = 16
 E = N // Q
 BLOCKS = M // P
-WARM_UPS = 10
 
 FLOPS = 2 * P * M * N
 
 BF16, F32, U16 = mybir.dt.bfloat16, mybir.dt.float32, mybir.dt.uint16
-MULT, ADD = mybir.AluOpType.mult, mybir.AluOpType.add
+ADD = mybir.AluOpType.add
+IDENTITY = mybir.ActivationFunctionType.Identity
 
 
 def tile_multiscalehead_kernel(tc, table, w, b, offs, out):
@@ -21,7 +21,7 @@ def tile_multiscalehead_kernel(tc, table, w, b, offs, out):
     with (
         tc.tile_pool(name="held", bufs=1) as held,
         tc.tile_pool(name="work", bufs=BLOCKS) as work,
-        tc.psum_pool(name="side_banks", bufs=1) as side_banks,
+        tc.psum_pool(name="bias_bank", bufs=1) as bias_bank,
         tc.psum_pool(name="banks", bufs=BLOCKS) as banks,
     ):
         offsets = held.tile([P, N // 16], U16, name="offsets")
@@ -33,15 +33,9 @@ def tile_multiscalehead_kernel(tc, table, w, b, offs, out):
         bias_rows = held.tile([BLOCKS, P], F32, name="bias_rows")
         nc.scalar.dma_start(bias_rows[:], b.rearrange("(t p) o -> t (p o)", p=P))
 
-        zeros = held.tile([P, N], BF16, name="zeros")
-        nc.vector.memset(zeros[:], 0.0)
-        unused = side_banks.tile([P, N], F32, name="unused")
-        for i in range(WARM_UPS):
-            nc.tensor.matmul(unused[:], zeros[:, 0:P], zeros[:], start=True, stop=True)
-
         identity = held.tile([BLOCKS, BLOCKS], F32, name="identity")
         make_identity(nc, identity[:])
-        bias_psum = side_banks.tile([P, BLOCKS], F32, name="bias_psum")
+        bias_psum = bias_bank.tile([P, BLOCKS], F32, name="bias_psum")
         nc.tensor.matmul(bias_psum[:], bias_rows[:], identity[:], start=True, stop=True)
         bias = held.tile([P, BLOCKS], F32, name="bias")
         nc.vector.tensor_copy(bias[:], bias_psum[:])
@@ -63,5 +57,5 @@ def tile_multiscalehead_kernel(tc, table, w, b, offs, out):
                 op=ADD,
             )
             scores = work.tile([P, E], F32, name="scores")
-            nc.vector.tensor_scalar(scores[:], sums[:], 1.0 / Q, bias[:, t : t + 1], op0=MULT, op1=ADD)
-            nc.sync.dma_start(out[t * P : (t + 1) * P, :], scores[:])
+            nc.scalar.activation(scores[:], sums[:], IDENTITY, bias=bias[:, t : t + 1], scale=1.0 / Q)
+            nc.scalar.dma_start(out[t * P : (t + 1) * P, :], scores[:])

@@ -8,12 +8,14 @@ N = 512
 Q = 16
 E = N // Q
 BLOCKS = M // P
+CHUNKS = 4
+CHUNK = S // CHUNKS
+WARM_UPS = 8
 
 FLOPS = 2 * P * M * N
 
 BF16, F32, U16 = mybir.dt.bfloat16, mybir.dt.float32, mybir.dt.uint16
-ADD = mybir.AluOpType.add
-IDENTITY = mybir.ActivationFunctionType.Identity
+MULT, ADD = mybir.AluOpType.mult, mybir.AluOpType.add
 
 
 def tile_multiscalehead_kernel(tc, table, w, b, offs, out):
@@ -21,24 +23,34 @@ def tile_multiscalehead_kernel(tc, table, w, b, offs, out):
     with (
         tc.tile_pool(name="held", bufs=1) as held,
         tc.tile_pool(name="work", bufs=BLOCKS) as work,
-        tc.psum_pool(name="bias_bank", bufs=1) as bias_bank,
+        tc.psum_pool(name="side_banks", bufs=1) as side_banks,
         tc.psum_pool(name="banks", bufs=BLOCKS) as banks,
     ):
         offsets = held.tile([P, N // 16], U16, name="offsets")
         nc.sync.dma_start(offsets[:], offs)
         states = held.tile([P, S], BF16, name="states")
-        nc.sync.dma_start(states[:], table)
+        for c in range(CHUNKS):
+            nc.sync.dma_start(states[:, c * CHUNK : (c + 1) * CHUNK], table[:, c * CHUNK : (c + 1) * CHUNK])
         weights = held.tile([P, M], BF16, name="weights")
         nc.scalar.dma_start(weights[:], w)
         bias_rows = held.tile([BLOCKS, P], F32, name="bias_rows")
         nc.scalar.dma_start(bias_rows[:], b.rearrange("(t p) o -> t (p o)", p=P))
 
+        zeros = held.tile([P, N], BF16, name="zeros")
+        nc.vector.memset(zeros[:], 0.0)
+        unused = side_banks.tile([P, N], F32, name="unused")
+        for i in range(WARM_UPS):
+            nc.tensor.matmul(unused[:], zeros[:, 0:P], zeros[:], start=True, stop=True)
+
         identity = held.tile([BLOCKS, BLOCKS], F32, name="identity")
         make_identity(nc, identity[:])
-        bias_psum = bias_bank.tile([P, BLOCKS], F32, name="bias_psum")
+        bias_psum = side_banks.tile([P, BLOCKS], F32, name="bias_psum")
         nc.tensor.matmul(bias_psum[:], bias_rows[:], identity[:], start=True, stop=True)
         bias = held.tile([P, BLOCKS], F32, name="bias")
         nc.vector.tensor_copy(bias[:], bias_psum[:])
+
+        for c in range(CHUNKS - 1):
+            nc.tensor.matmul(unused[:], weights[:, 0:P], states[:, c * CHUNK : c * CHUNK + N], start=True, stop=True)
 
         for t in range(BLOCKS):
             projected = banks.tile([P, N], F32, name="projected")
@@ -57,5 +69,5 @@ def tile_multiscalehead_kernel(tc, table, w, b, offs, out):
                 op=ADD,
             )
             scores = work.tile([P, E], F32, name="scores")
-            nc.scalar.activation(scores[:], sums[:], IDENTITY, bias=bias[:, t : t + 1], scale=1.0 / Q)
-            nc.scalar.dma_start(out[t * P : (t + 1) * P, :], scores[:])
+            nc.vector.tensor_scalar(scores[:], sums[:], 1.0 / Q, bias[:, t : t + 1], op0=MULT, op1=ADD)
+            nc.sync.dma_start(out[t * P : (t + 1) * P, :], scores[:])

@@ -8,9 +8,6 @@ N = 512
 Q = 16
 E = N // Q
 BLOCKS = M // P
-CHUNKS = 4
-CHUNK = S // CHUNKS
-WARM_UPS = 8
 
 FLOPS = 2 * P * M * N
 
@@ -23,51 +20,46 @@ def tile_multiscalehead_kernel(tc, table, w, b, offs, out):
     with (
         tc.tile_pool(name="held", bufs=1) as held,
         tc.tile_pool(name="work", bufs=BLOCKS) as work,
-        tc.psum_pool(name="side_banks", bufs=1) as side_banks,
+        tc.psum_pool(name="bias_bank", bufs=1) as bias_bank,
         tc.psum_pool(name="banks", bufs=BLOCKS) as banks,
     ):
         offsets = held.tile([P, N // 16], U16, name="offsets")
         nc.sync.dma_start(offsets[:], offs)
         states = held.tile([P, S], BF16, name="states")
-        for c in range(CHUNKS):
-            nc.sync.dma_start(states[:, c * CHUNK : (c + 1) * CHUNK], table[:, c * CHUNK : (c + 1) * CHUNK])
+        nc.sync.dma_start(states[:], table)
         weights = held.tile([P, M], BF16, name="weights")
         nc.scalar.dma_start(weights[:], w)
         bias_rows = held.tile([BLOCKS, P], F32, name="bias_rows")
         nc.scalar.dma_start(bias_rows[:], b.rearrange("(t p) o -> t (p o)", p=P))
 
-        zeros = held.tile([P, N], BF16, name="zeros")
-        nc.vector.memset(zeros[:], 0.0)
-        unused = side_banks.tile([P, N], F32, name="unused")
-        for i in range(WARM_UPS):
-            nc.tensor.matmul(unused[:], zeros[:, 0:P], zeros[:], start=True, stop=True)
-
         identity = held.tile([BLOCKS, BLOCKS], F32, name="identity")
         make_identity(nc, identity[:])
-        bias_psum = side_banks.tile([P, BLOCKS], F32, name="bias_psum")
+        bias_psum = bias_bank.tile([P, BLOCKS], F32, name="bias_psum")
         nc.tensor.matmul(bias_psum[:], bias_rows[:], identity[:], start=True, stop=True)
         bias = held.tile([P, BLOCKS], F32, name="bias")
         nc.vector.tensor_copy(bias[:], bias_psum[:])
 
-        for c in range(CHUNKS - 1):
-            nc.tensor.matmul(unused[:], weights[:, 0:P], states[:, c * CHUNK : c * CHUNK + N], start=True, stop=True)
-
-        for t in range(BLOCKS):
-            projected = banks.tile([P, N], F32, name="projected")
-            nc.tensor.matmul(
-                projected[:],
-                weights[:, t * P : (t + 1) * P],
-                states[:].indirect(offsets[:]),
-                start=True,
-                stop=True,
-            )
-            sums = work.tile([P, E], F32, name="sums")
-            nc.vector.tensor_reduce(
-                sums[:],
-                projected[:].rearrange("p (e q) -> p e q", q=Q),
-                axis=mybir.AxisListType.X,
-                op=ADD,
-            )
-            scores = work.tile([P, E], F32, name="scores")
-            nc.vector.tensor_scalar(scores[:], sums[:], 1.0 / Q, bias[:, t : t + 1], op0=MULT, op1=ADD)
-            nc.sync.dma_start(out[t * P : (t + 1) * P, :], scores[:])
+        sums = [None] * BLOCKS
+        for t in range(BLOCKS + 1):
+            if t < BLOCKS:
+                projected = banks.tile([P, N], F32, name="projected")
+                nc.tensor.matmul(
+                    projected[:],
+                    weights[:, t * P : (t + 1) * P],
+                    states[:].indirect(offsets[:]),
+                    start=True,
+                    stop=True,
+                )
+                sums[t] = work.tile([P, E], F32, name="sums")
+                nc.vector.tensor_reduce(
+                    sums[t][:],
+                    projected[:].rearrange("p (e q) -> p e q", q=Q),
+                    axis=mybir.AxisListType.X,
+                    op=ADD,
+                )
+            if t > 0:
+                scores = work.tile([P, E], F32, name="scores")
+                nc.vector.tensor_scalar(
+                    scores[:], sums[t - 1][:], 1.0 / Q, bias[:, t - 1 : t], op0=MULT, op1=ADD
+                )
+                nc.sync.dma_start(out[(t - 1) * P : t * P, :], scores[:])

@@ -12,7 +12,8 @@ BLOCKS = M // P
 FLOPS = 2 * P * M * N
 
 BF16, F32, U16 = mybir.dt.bfloat16, mybir.dt.float32, mybir.dt.uint16
-MULT, ADD = mybir.AluOpType.mult, mybir.AluOpType.add
+ADD = mybir.AluOpType.add
+IDENTITY = mybir.ActivationFunctionType.Identity
 
 
 def tile_multiscalehead_kernel(tc, table, w, b, offs, out):
@@ -28,9 +29,9 @@ def tile_multiscalehead_kernel(tc, table, w, b, offs, out):
         states = held.tile([P, S], BF16, name="states")
         nc.sync.dma_start(states[:], table)
         weights = held.tile([P, M], BF16, name="weights")
-        nc.scalar.dma_start(weights[:], w)
+        nc.gpsimd.dma_start(weights[:], w)
         bias_rows = held.tile([BLOCKS, P], F32, name="bias_rows")
-        nc.scalar.dma_start(bias_rows[:], b.rearrange("(t p) o -> t (p o)", p=P))
+        nc.gpsimd.dma_start(bias_rows[:], b.rearrange("(t p) o -> t (p o)", p=P))
 
         identity = held.tile([BLOCKS, BLOCKS], F32, name="identity")
         make_identity(nc, identity[:])
@@ -39,27 +40,22 @@ def tile_multiscalehead_kernel(tc, table, w, b, offs, out):
         bias = held.tile([P, BLOCKS], F32, name="bias")
         nc.vector.tensor_copy(bias[:], bias_psum[:])
 
-        sums = [None] * BLOCKS
-        for t in range(BLOCKS + 1):
-            if t < BLOCKS:
-                projected = banks.tile([P, N], F32, name="projected")
-                nc.tensor.matmul(
-                    projected[:],
-                    weights[:, t * P : (t + 1) * P],
-                    states[:].indirect(offsets[:]),
-                    start=True,
-                    stop=True,
-                )
-                sums[t] = work.tile([P, E], F32, name="sums")
-                nc.vector.tensor_reduce(
-                    sums[t][:],
-                    projected[:].rearrange("p (e q) -> p e q", q=Q),
-                    axis=mybir.AxisListType.X,
-                    op=ADD,
-                )
-            if t > 0:
-                scores = work.tile([P, E], F32, name="scores")
-                nc.vector.tensor_scalar(
-                    scores[:], sums[t - 1][:], 1.0 / Q, bias[:, t - 1 : t], op0=MULT, op1=ADD
-                )
-                nc.sync.dma_start(out[(t - 1) * P : t * P, :], scores[:])
+        for t in range(BLOCKS):
+            projected = banks.tile([P, N], F32, name="projected")
+            nc.tensor.matmul(
+                projected[:],
+                weights[:, t * P : (t + 1) * P],
+                states[:].indirect(offsets[:]),
+                start=True,
+                stop=True,
+            )
+            sums = work.tile([P, E], F32, name="sums")
+            nc.vector.tensor_reduce(
+                sums[:],
+                projected[:].rearrange("p (e q) -> p e q", q=Q),
+                axis=mybir.AxisListType.X,
+                op=ADD,
+            )
+            scores = work.tile([P, E], F32, name="scores")
+            nc.scalar.activation(scores[:], sums[:], IDENTITY, bias=bias[:, t : t + 1], scale=1.0 / Q)
+            nc.scalar.dma_start(out[t * P : (t + 1) * P, :], scores[:])

@@ -26,10 +26,10 @@ def tile_multiscalehead_kernel(tc, table, w, b, offs, out):
     ):
         offsets = held.tile([P, N // 16], U16, name="offsets")
         nc.sync.dma_start(offsets[:], offs)
+        weights = held.tile([P, M], BF16, name="weights")
+        nc.sync.dma_start(weights[:], w)
         states = held.tile([P, S], BF16, name="states")
         nc.sync.dma_start(states[:], table)
-        weights = held.tile([P, M], BF16, name="weights")
-        nc.gpsimd.dma_start(weights[:], w)
         bias_rows = held.tile([BLOCKS, P], F32, name="bias_rows")
         nc.gpsimd.dma_start(bias_rows[:], b.rearrange("(t p) o -> t (p o)", p=P))
 

@@ -8,6 +8,9 @@ N = 512
 Q = 16
 E = N // Q
 BLOCKS = M // P
+PIECE = 256
+PIECES = N // PIECE
+PSUM_BANKS = 8
 
 FLOPS = 2 * P * M * N
 
@@ -22,7 +25,7 @@ def tile_multiscalehead_kernel(tc, table, w, b, offs, out):
         tc.tile_pool(name="held", bufs=1) as held,
         tc.tile_pool(name="work", bufs=BLOCKS) as work,
         tc.psum_pool(name="bias_bank", bufs=1) as bias_bank,
-        tc.psum_pool(name="banks", bufs=BLOCKS) as banks,
+        tc.psum_pool(name="banks", bufs=PSUM_BANKS - 1) as banks,
     ):
         offsets = held.tile([P, N // 16], U16, name="offsets")
         nc.sync.dma_start(offsets[:], offs)
@@ -41,21 +44,22 @@ def tile_multiscalehead_kernel(tc, table, w, b, offs, out):
         nc.vector.tensor_copy(bias[:], bias_psum[:])
 
         for t in range(BLOCKS):
-            projected = banks.tile([P, N], F32, name="projected")
-            nc.tensor.matmul(
-                projected[:],
-                weights[:, t * P : (t + 1) * P],
-                states[:].indirect(offsets[:]),
-                start=True,
-                stop=True,
-            )
             sums = work.tile([P, E], F32, name="sums")
-            nc.vector.tensor_reduce(
-                sums[:],
-                projected[:].rearrange("p (e q) -> p e q", q=Q),
-                axis=mybir.AxisListType.X,
-                op=ADD,
-            )
+            for h in range(PIECES):
+                projected = banks.tile([P, PIECE], F32, name="projected")
+                nc.tensor.matmul(
+                    projected[:],
+                    weights[:, t * P : (t + 1) * P],
+                    states[:].indirect(offsets[:, h * (PIECE // 16) : (h + 1) * (PIECE // 16)]),
+                    start=True,
+                    stop=True,
+                )
+                nc.vector.tensor_reduce(
+                    sums[:, h * (PIECE // Q) : (h + 1) * (PIECE // Q)],
+                    projected[:].rearrange("p (e q) -> p e q", q=Q),
+                    axis=mybir.AxisListType.X,
+                    op=ADD,
+                )
             scores = work.tile([P, E], F32, name="scores")
             nc.scalar.activation(scores[:], sums[:], IDENTITY, bias=bias[:, t : t + 1], scale=1.0 / Q)
             nc.scalar.dma_start(out[t * P : (t + 1) * P, :], scores[:])

@@ -43,6 +43,9 @@ def tile_multiscalehead_kernel(tc, table, w, b, offs, out):
         bias = held.tile([P, BLOCKS], F32, name="bias")
         nc.vector.tensor_copy(bias[:], bias_psum[:])
 
+        scores = held.tile([P, BLOCKS, E], F32, name="scores")
+        out_blocks = out.rearrange("(t p) e -> p t e", p=P)
+
         for t in range(BLOCKS):
             sums = work.tile([P, E], F32, name="sums")
             for h in range(PIECES):
@@ -60,6 +63,8 @@ def tile_multiscalehead_kernel(tc, table, w, b, offs, out):
                     axis=mybir.AxisListType.X,
                     op=ADD,
                 )
-            scores = work.tile([P, E], F32, name="scores")
-            nc.scalar.activation(scores[:], sums[:], IDENTITY, bias=bias[:, t : t + 1], scale=1.0 / Q)
-            nc.scalar.dma_start(out[t * P : (t + 1) * P, :], scores[:])
+            nc.scalar.activation(scores[:, t, :], sums[:], IDENTITY, bias=bias[:, t : t + 1], scale=1.0 / Q)
+            if t == BLOCKS - 2:
+                nc.scalar.dma_start(out_blocks[:, 0 : BLOCKS - 1, :], scores[:, 0 : BLOCKS - 1, :])
+            if t == BLOCKS - 1:
+                nc.scalar.dma_start(out_blocks[:, BLOCKS - 1, :], scores[:, BLOCKS - 1, :])

@@ -1,5 +1,4 @@
 import concourse.mybir as mybir
-from concourse.masks import make_identity
 
 P = 128
 S = 4096
@@ -15,56 +14,53 @@ PSUM_BANKS = 8
 FLOPS = 2 * P * M * N
 
 BF16, F32, U16 = mybir.dt.bfloat16, mybir.dt.float32, mybir.dt.uint16
-ADD = mybir.AluOpType.add
-IDENTITY = mybir.ActivationFunctionType.Identity
+ADD, MULT = mybir.AluOpType.add, mybir.AluOpType.mult
 
 
 def tile_multiscalehead_kernel(tc, table, w, b, offs, out):
     nc = tc.nc
     with (
         tc.tile_pool(name="held", bufs=1) as held,
-        tc.tile_pool(name="work", bufs=BLOCKS) as work,
-        tc.psum_pool(name="bias_bank", bufs=1) as bias_bank,
-        tc.psum_pool(name="banks", bufs=PSUM_BANKS - 1) as banks,
+        tc.psum_pool(name="banks", bufs=PSUM_BANKS) as banks,
     ):
+
         offsets = held.tile([P, N // 16], U16, name="offsets")
         nc.sync.dma_start(offsets[:], offs)
-        weights = held.tile([P, M], BF16, name="weights")
-        nc.sync.dma_start(weights[:], w)
+        loaded_weights = held.tile([P, M], BF16, name="loaded_weights")
+        nc.sync.dma_start(loaded_weights[:], w)
         states = held.tile([P, S], BF16, name="states")
         nc.sync.dma_start(states[:], table)
-        bias_rows = held.tile([BLOCKS, P], F32, name="bias_rows")
-        nc.gpsimd.dma_start(bias_rows[:], b.rearrange("(t p) o -> t (p o)", p=P))
-
-        identity = held.tile([BLOCKS, BLOCKS], F32, name="identity")
-        make_identity(nc, identity[:])
-        bias_psum = bias_bank.tile([P, BLOCKS], F32, name="bias_psum")
-        nc.tensor.matmul(bias_psum[:], bias_rows[:], identity[:], start=True, stop=True)
         bias = held.tile([P, BLOCKS], F32, name="bias")
-        nc.vector.tensor_copy(bias[:], bias_psum[:])
+        nc.sync.dma_start(bias[:], b.rearrange("(p t) o -> p (t o)", t=BLOCKS))
 
-        scores = held.tile([P, BLOCKS, E], F32, name="scores")
-        out_blocks = out.rearrange("(t p) e -> p t e", p=P)
+        weights = held.tile([P, BLOCKS, P], BF16, name="weights")
+        nc.vector.tensor_copy(weights[:], loaded_weights[:].rearrange("k (p t) -> k t p", t=BLOCKS))
 
+        sums = held.tile([P, BLOCKS, E], F32, name="sums")
         for t in range(BLOCKS):
-            sums = work.tile([P, E], F32, name="sums")
             for h in range(PIECES):
                 projected = banks.tile([P, PIECE], F32, name="projected")
                 nc.tensor.matmul(
                     projected[:],
-                    weights[:, t * P : (t + 1) * P],
+                    weights[:, t, :],
                     states[:].indirect(offsets[:, h * (PIECE // 16) : (h + 1) * (PIECE // 16)]),
                     start=True,
                     stop=True,
                 )
                 nc.vector.tensor_reduce(
-                    sums[:, h * (PIECE // Q) : (h + 1) * (PIECE // Q)],
+                    sums[:, t, h * (PIECE // Q) : (h + 1) * (PIECE // Q)],
                     projected[:].rearrange("p (e q) -> p e q", q=Q),
                     axis=mybir.AxisListType.X,
                     op=ADD,
                 )
-            nc.scalar.activation(scores[:, t, :], sums[:], IDENTITY, bias=bias[:, t : t + 1], scale=1.0 / Q)
-            if t == BLOCKS - 2:
-                nc.scalar.dma_start(out_blocks[:, 0 : BLOCKS - 1, :], scores[:, 0 : BLOCKS - 1, :])
-            if t == BLOCKS - 1:
-                nc.scalar.dma_start(out_blocks[:, BLOCKS - 1, :], scores[:, BLOCKS - 1, :])
+
+        scores = held.tile([P, BLOCKS, E], F32, name="scores")
+        nc.vector.scalar_tensor_tensor(
+            scores[:],
+            sums[:],
+            1.0 / Q,
+            bias[:].unsqueeze(2).to_broadcast([P, BLOCKS, E]),
+            op0=MULT,
+            op1=ADD,
+        )
+        nc.sync.dma_start(out.rearrange("(p t) e -> p (t e)", t=BLOCKS), scores[:].rearrange("p t e -> p (t e)"))

@@ -14,7 +14,8 @@ PSUM_BANKS = 8
 FLOPS = 2 * P * M * N
 
 BF16, F32, U16 = mybir.dt.bfloat16, mybir.dt.float32, mybir.dt.uint16
-ADD, MULT = mybir.AluOpType.add, mybir.AluOpType.mult
+ADD = mybir.AluOpType.add
+IDENTITY = mybir.ActivationFunctionType.Identity
 
 
 def tile_multiscalehead_kernel(tc, table, w, b, offs, out):
@@ -37,6 +38,7 @@ def tile_multiscalehead_kernel(tc, table, w, b, offs, out):
         nc.vector.tensor_copy(weights[:], loaded_weights[:].rearrange("k (p t) -> k t p", t=BLOCKS))
 
         sums = held.tile([P, BLOCKS, E], F32, name="sums")
+        scores = held.tile([P, BLOCKS, E], F32, name="scores")
         for t in range(BLOCKS):
             for h in range(PIECES):
                 projected = banks.tile([P, PIECE], F32, name="projected")
@@ -53,14 +55,6 @@ def tile_multiscalehead_kernel(tc, table, w, b, offs, out):
                     axis=mybir.AxisListType.X,
                     op=ADD,
                 )
+            nc.scalar.activation(scores[:, t, :], sums[:, t, :], IDENTITY, bias=bias[:, t : t + 1], scale=1.0 / Q)
 
-        scores = held.tile([P, BLOCKS, E], F32, name="scores")
-        nc.vector.scalar_tensor_tensor(
-            scores[:],
-            sums[:],
-            1.0 / Q,
-            bias[:].unsqueeze(2).to_broadcast([P, BLOCKS, E]),
-            op0=MULT,
-            op1=ADD,
-        )
         nc.sync.dma_start(out.rearrange("(p t) e -> p (t e)", t=BLOCKS), scores[:].rearrange("p t e -> p (t e)"))

@@ -32,7 +32,7 @@ def tile_multiscalehead_kernel(tc, table, w, b, offs, out):
         states = held.tile([P, S], BF16, name="states")
         nc.sync.dma_start(states[:], table)
         bias = held.tile([P, BLOCKS], F32, name="bias")
-        nc.sync.dma_start(bias[:], b.rearrange("(p t) o -> p (t o)", t=BLOCKS))
+        nc.gpsimd.dma_start(bias[:], b.rearrange("(p t) o -> p (t o)", t=BLOCKS))
 
         weights = held.tile([P, BLOCKS, P], BF16, name="weights")
         nc.vector.tensor_copy(weights[:], loaded_weights[:].rearrange("k (p t) -> k t p", t=BLOCKS))

@@ -27,15 +27,14 @@ def tile_multiscalehead_kernel(tc, table, w, b, offs, out):
 
         offsets = held.tile([P, N // 16], U16, name="offsets")
         nc.sync.dma_start(offsets[:], offs)
-        loaded_weights = held.tile([P, M], BF16, name="loaded_weights")
-        nc.sync.dma_start(loaded_weights[:], w)
+        weights = held.tile([P, M], BF16, name="weights")
+        nc.sync.dma_start(weights[:], w)
         states = held.tile([P, S], BF16, name="states")
         nc.sync.dma_start(states[:], table)
         bias = held.tile([P, BLOCKS], F32, name="bias")
         nc.gpsimd.dma_start(bias[:], b.rearrange("(p t) o -> p (t o)", t=BLOCKS))
 
-        weights = held.tile([P, BLOCKS, P], BF16, name="weights")
-        nc.vector.tensor_copy(weights[:], loaded_weights[:].rearrange("k (p t) -> k t p", t=BLOCKS))
+        block_weights = weights[:].rearrange("k (p t) -> k t p", t=BLOCKS)
 
         sums = held.tile([P, BLOCKS, E], F32, name="sums")
         scores = held.tile([P, BLOCKS, E], F32, name="scores")
@@ -44,7 +43,7 @@ def tile_multiscalehead_kernel(tc, table, w, b, offs, out):
                 projected = banks.tile([P, PIECE], F32, name="projected")
                 nc.tensor.matmul(
                     projected[:],
-                    weights[:, t, :],
+                    block_weights[:, t, :],
                     states[:].indirect(offsets[:, h * (PIECE // 16) : (h + 1) * (PIECE // 16)]),
                     start=True,
                     stop=True,

@@ -25,12 +25,12 @@ def tile_multiscalehead_kernel(tc, table, w, b, offs, out):
         tc.psum_pool(name="banks", bufs=PSUM_BANKS) as banks,
     ):
 
+        states = held.tile([P, S], BF16, name="states")
+        nc.sync.dma_start(states[:], table)
         offsets = held.tile([P, N // 16], U16, name="offsets")
         nc.sync.dma_start(offsets[:], offs)
         weights = held.tile([P, M], BF16, name="weights")
         nc.sync.dma_start(weights[:], w)
-        states = held.tile([P, S], BF16, name="states")
-        nc.sync.dma_start(states[:], table)
         bias = held.tile([P, BLOCKS], F32, name="bias")
         nc.gpsimd.dma_start(bias[:], b.rearrange("(p t) o -> p (t o)", t=BLOCKS))
 

@@ -32,7 +32,7 @@ def tile_multiscalehead_kernel(tc, table, w, b, offs, out):
         weights = held.tile([P, M], BF16, name="weights")
         nc.sync.dma_start(weights[:], w)
         bias = held.tile([P, BLOCKS], F32, name="bias")
-        nc.gpsimd.dma_start(bias[:], b.rearrange("(p t) o -> p (t o)", t=BLOCKS))
+        nc.scalar.dma_start(bias[:], b.rearrange("(p t) o -> p (t o)", t=BLOCKS))
 
         block_weights = weights[:].rearrange("k (p t) -> k t p", t=BLOCKS)
 

import concourse.mybir as mybir

P = 128
S = 4096
M = 512
N = 512
Q = 16
E = N // Q
BLOCKS = M // P
PIECE = 256
PIECES = N // PIECE
PSUM_BANKS = 8

FLOPS = 2 * P * M * N

BF16, F32, U16 = mybir.dt.bfloat16, mybir.dt.float32, mybir.dt.uint16
ADD = mybir.AluOpType.add
IDENTITY = mybir.ActivationFunctionType.Identity


def tile_multiscalehead_kernel(tc, table, w, b, offs, out):
    nc = tc.nc
    with (
        tc.tile_pool(name="held", bufs=1) as held,
        tc.psum_pool(name="banks", bufs=PSUM_BANKS) as banks,
    ):

        states = held.tile([P, S], BF16, name="states")
        nc.sync.dma_start(states[:], table)
        offsets = held.tile([P, N // 16], U16, name="offsets")
        nc.sync.dma_start(offsets[:], offs)
        weights = held.tile([P, M], BF16, name="weights")
        nc.sync.dma_start(weights[:], w)
        bias = held.tile([P, BLOCKS], F32, name="bias")
        nc.scalar.dma_start(bias[:], b.rearrange("(p t) o -> p (t o)", t=BLOCKS))

        block_weights = weights[:].rearrange("k (p t) -> k t p", t=BLOCKS)

        sums = held.tile([P, BLOCKS, E], F32, name="sums")
        scores = held.tile([P, BLOCKS, E], F32, name="scores")
        for t in range(BLOCKS):
            for h in range(PIECES):
                projected = banks.tile([P, PIECE], F32, name="projected")
                nc.tensor.matmul(
                    projected[:],
                    block_weights[:, t, :],
                    states[:].indirect(offsets[:, h * (PIECE // 16) : (h + 1) * (PIECE // 16)]),
                    start=True,
                    stop=True,
                )
                nc.vector.tensor_reduce(
                    sums[:, t, h * (PIECE // Q) : (h + 1) * (PIECE // Q)],
                    projected[:].rearrange("p (e q) -> p e q", q=Q),
                    axis=mybir.AxisListType.X,
                    op=ADD,
                )
            nc.scalar.activation(scores[:, t, :], sums[:, t, :], IDENTITY, bias=bias[:, t : t + 1], scale=1.0 / Q)

        nc.sync.dma_start(out.rearrange("(p t) e -> p (t e)", t=BLOCKS), scores[:].rearrange("p t e -> p (t e)"))
